import numpy as np
import ml_dtypes


def mxq(x, axis, fmt="e4m3"):
    dtype, down = {"e4m3": (ml_dtypes.float8_e4m3fn, 7), "e5m2": (ml_dtypes.float8_e5m2, 14)}[fmt]
    v = np.moveaxis(np.asarray(x, np.float32).astype(ml_dtypes.bfloat16).astype(np.float64), axis, -1)
    blocks = v.reshape(v.shape[:-1] + (-1, 32))
    amax = np.abs(blocks).max(-1, keepdims=True)
    byte = np.maximum(np.where(amax > 0, np.frexp(amax)[1] - 1 + 127, 0) - down, 1)
    scale = np.exp2(byte - 127.0)
    codes = (blocks / scale).astype(np.float32).astype(dtype).astype(np.float64)
    return np.moveaxis((codes * scale).reshape(v.shape), -1, axis)


WIDE = False


def mx_kscale(k):
    if not WIDE:
        return np.ones(k)
    levels = np.array([10, -10, 5, -5, 0])
    if k % 512:
        return np.exp2(np.random.permutation(np.resize(levels, k // 32))).repeat(32)
    a = np.empty((k // 512, 16))
    for p in range(k // 512):
        a[p, :8] = np.random.permutation(np.resize(levels, 8))
        for g in range(8):
            far = levels[np.abs(levels - a[p, g]) >= 10]
            a[p, g + 8] = far[np.random.randint(len(far))]
    return np.exp2(a.ravel()).repeat(32)


BF16 = ml_dtypes.bfloat16


def bf(x):
    return np.asarray(x, np.float32).astype(BF16)


def f64(x):
    return np.asarray(x).astype(np.float64)


B, S, T, E, D, H = 1, 512, 512, 2048, 2048, 16
DK = D // H


def rope_tables(n):
    m = np.arange(n, dtype=np.float64)[:, None]
    i = np.repeat(np.arange(DK // 2, dtype=np.float64), 2)[None, :]
    ang = m * np.exp(-(2.0 * np.log(1e4) / DK) * i)
    return np.cos(ang), np.sin(ang)


def rotate_pairs(x):
    return np.stack([-x[..., 1::2], x[..., 0::2]], axis=-1).reshape(x.shape)


def setup_inputs():
    s = mx_kscale(E)
    return {"x": bf(np.random.standard_normal((B, S, E)) * s),
            "w": bf(np.random.standard_normal((E, D)) * 1.1 / np.sqrt(E) / s[:, None]),
            "b": bf(np.random.standard_normal(D) * 0.4)}


def core(x, w, b):
    p = (mxq(f64(x), 2, "e4m3") @ mxq(f64(w), 0, "e4m3")) + f64(b)
    p = p.reshape(B, S, H, DK).transpose(0, 2, 1, 3)
    r1, r2 = rope_tables(S)
    return p * r1 + rotate_pairs(p) * r2


def e4m3fn_bytes(y):
    return np.clip(np.asarray(y, np.float64), -448.0, 448.0).astype(np.float32).astype(ml_dtypes.float8_e4m3fn).view(np.uint8)


def reference(x, w, b):
    out = core(x, w, b)
    s = np.max(np.abs(out)) / 448.0
    return out, e4m3fn_bytes(out / s)

@@ -1,0 +1,311 @@
+from contextlib import ExitStack
+
+import concourse.mybir as mybir
+from concourse.masks import make_identity
+
+FLOPS = 2 * 512 * 2048 * 2048
+
+F32 = mybir.dt.float32
+BF16 = mybir.dt.bfloat16
+I32 = mybir.dt.int32
+U32 = mybir.dt.uint32
+U8 = mybir.dt.uint8
+FP8X4 = mybir.dt.float8_e4m3fn_x4
+FP8 = mybir.dt.float8_e4m3fn
+ALU = mybir.AluOpType
+ACT = mybir.ActivationFunctionType
+AX = mybir.AxisListType
+
+P = 128
+PASSES = 4
+UNITS = 8
+W_RANGES = ((0, 256), (256, 256), (512, 512), (1024, 512), (1536, 512))
+V_SHARE = 1344
+TWO_PI = 6.283185307179586
+
+
+def tile_multiheadedattention_pa_kernel(tc, x, w, b, out_0, out_1):
+    nc = tc.nc
+    with ExitStack() as ctx:
+        const = ctx.enter_context(tc.tile_pool(name="const", bufs=1))
+        work = ctx.enter_context(tc.tile_pool(name="work", bufs=2))
+        psum = ctx.enter_context(tc.psum_pool(name="psum", bufs=4))
+        ctx.enter_context(tc.manual_schedule())
+
+        xv = x[0].rearrange("(r a) k -> r a k", a=4)
+        o0v = out_0[0].rearrange("h (r a) j -> r h (a j)", a=4)
+        o1v = out_1[0].rearrange("h (r a) j -> r h (a j)", a=4)
+
+        b16 = const.tile([16, P], BF16, name="b16")
+        nc.sync.dma_start(out=b16[:], in_=b.rearrange("(h c) -> h c", c=P))
+        wraw = {}
+        xs = {}
+
+        def load_w(c0, width):
+            for g in range(PASSES):
+                t = const.tile([P, 4, width], BF16, name="wr%d_%d" % (c0, g))
+                nc.sync.dma_start(
+                    out=t[:],
+                    in_=w[512 * g : 512 * (g + 1), c0 : c0 + width].rearrange("(p j) n -> p j n", j=4),
+                )
+                wraw[(c0, g)] = t
+
+        load_w(W_RANGES[0][0], W_RANGES[0][1])
+        for g in range(PASSES):
+            t = const.tile([P, 4, 512], BF16, name="xs%d" % g)
+            nc.sync.dma_start(out=t[:], in_=xv[:, :, 512 * g : 512 * (g + 1)])
+            xs[g] = t
+        for c0, width in W_RANGES[1:]:
+            load_w(c0, width)
+
+        def raw(u, g):
+            col = 256 * u
+            for c0, width in W_RANGES:
+                if c0 <= col < c0 + width:
+                    return wraw[(c0, g)][:, :, col - c0 : col - c0 + 256]
+            return None
+
+        ident = const.tile([P, P], F32, name="ident")
+        swap = const.tile([P, P], F32, name="swap")
+        m_idx = const.tile([P, 512], I32, name="m_idx")
+        p_idx = const.tile([P, 1], I32, name="p_idx")
+        par = const.tile([P, 1], I32, name="par")
+        sgn = const.tile([P, 1], F32, name="sgn")
+        zero = const.tile([P, 1], F32, name="zero")
+        warm = const.tile([P, 1], F32, name="warm")
+        freq = const.tile([P, P], F32, name="freq")
+        turns = const.tile([P, P], F32, name="turns")
+        b32 = const.tile([P, P], F32, name="b32")
+        ucol = const.tile([P, 1], F32, name="ucol")
+        bias = const.tile([P, 16], F32, name="bias")
+        cos_t = const.tile([P, 512], F32, name="cos_t")
+        sin_t = const.tile([P, 512], F32, name="sin_t")
+        out_sb = const.tile([P, 16 * 512], F32, name="out_sb")
+        o8 = const.tile([P, 16 * 512], FP8, name="o8")
+        pm = const.tile([P, 16], F32, name="pm")
+        pmax = const.tile([P, 1], F32, name="pmax")
+        amax = const.tile([P, 1], F32, name="amax")
+        rec = const.tile([P, 1], F32, name="rec")
+        fac = const.tile([P, 1], F32, name="fac")
+
+        make_identity(nc, ident[:])
+        nc.gpsimd.iota(m_idx[:], pattern=[[1, 4], [4, P]], base=0, channel_multiplier=0)
+        nc.gpsimd.iota(p_idx[:], pattern=[[0, 1]], base=0, channel_multiplier=1)
+
+        nc.vector.memset(zero[:], 0.0)
+        nc.scalar.activation(out=warm[:], in_=zero[:], func=ACT.Sin)
+        nc.vector.memset(freq[:, 0:2], 1.0)
+        nc.vector.memset(b32[:], 0.0)
+        for s in range(6):
+            n = 2 << s
+            nc.vector.tensor_scalar(
+                out=freq[:, n : 2 * n], in0=freq[:, 0:n],
+                scalar1=10000.0 ** (-(n // 2) / 64.0), scalar2=None, op0=ALU.mult,
+            )
+        nc.vector.tensor_scalar(out=turns[:], in0=freq[:], scalar1=1.0 / TWO_PI, scalar2=None, op0=ALU.mult)
+        nc.vector.tensor_copy(out=b32[0:16, :], in_=b16[:])
+        pc = psum.tile([P, 512], F32, tag="t", name="pc")
+        nc.tensor.transpose(out=pc[:, 0:P], in_=turns[:], identity=ident[:])
+        nc.tensor.transpose(out=pc[:, P : 2 * P], in_=b32[:], identity=ident[:])
+        nc.vector.tensor_copy(out=ucol[:], in_=pc[:, 0:1])
+        nc.vector.tensor_copy(out=bias[:], in_=pc[:, P : P + 16])
+        idv = ident[:].rearrange("p (i e) -> p i e", e=2)
+        swv = swap[:].rearrange("p (i e) -> p i e", e=2)
+        nc.vector.tensor_copy(out=swv[:, :, 0:1], in_=idv[:, :, 1:2])
+        nc.vector.tensor_copy(out=swv[:, :, 1:2], in_=idv[:, :, 0:1])
+        nc.vector.tensor_scalar(out=par[:], in0=p_idx[:], scalar1=1, scalar2=None, op0=ALU.bitwise_and)
+        nc.vector.tensor_scalar(out=sgn[:], in0=par[:], scalar1=-2.0, scalar2=1.0, op0=ALU.mult, op1=ALU.add)
+
+        wg = {}
+        wq = {}
+        wsc = {}
+        zt = {}
+        prod_t = {}
+        ot = {}
+        xt = {}
+        xg = {}
+        xq = {}
+        xsc = {}
+
+        def interleave(eng, u, half):
+            t = work.tile([P, 2, 256, 4], BF16, tag="wg%d" % half, name="wg%d_%d" % (half, u),
+                          bufs=(2 if half == 0 else 1), align_bytes=64)
+            wg[(u, half)] = t
+            for gg in range(2):
+                src = raw(u, 2 * half + gg).rearrange("p j c -> p c j")
+                dst = t[:, gg, :, :]
+                if eng == "S":
+                    nc.scalar.copy(out=dst, in_=src)
+                elif eng == "G":
+                    nc.gpsimd.tensor_scalar(out=dst, in0=src, scalar1=1.0, scalar2=0.0, op0=ALU.mult, op1=ALU.add)
+                else:
+                    nc.vector.tensor_copy(out=dst, in_=src)
+
+        def quant(u):
+            q = work.tile([P, PASSES, 256], U32, tag="wq", name="wq%d" % u, bufs=3, align_bytes=64)
+            s = work.tile([P, PASSES, 256], U8, tag="wsc", name="wsc%d" % u, bufs=3, align_bytes=64)
+            wq[u] = q
+            wsc[u] = s
+            for half in range(2):
+                nc.vector.quantize_mx(
+                    out=q[:, 2 * half : 2 * half + 2, :].rearrange("p g c -> p (g c)").bitcast(FP8X4),
+                    scales=s[:, 2 * half : 2 * half + 2, :].rearrange("p g c -> p (g c)"),
+                    in_=wg[(u, half)][:].rearrange("p g c j -> p (g c j)"),
+                )
+
+        def mm_pass(u, hh, g):
+            nc.tensor.matmul_mx(
+                out=zt[(u, hh)][:],
+                lhsT=wq[u][:, g, P * hh : P * (hh + 1)].bitcast(FP8X4),
+                lhsT_scale=wsc[u][:, g, P * hh : P * (hh + 1)],
+                rhs=xq[g][:].bitcast(FP8X4),
+                rhs_scale=xsc[g][:],
+                start=(g == 0),
+                stop=(g == PASSES - 1),
+            )
+
+        def mm(u, g_outer):
+            for hh in range(2):
+                zt[(u, hh)] = psum.tile([P, 512], F32, tag="z", name="z%d_%d" % (u, hh))
+            if g_outer:
+                for g in range(PASSES):
+                    for hh in range(2):
+                        mm_pass(u, hh, g)
+            else:
+                for hh in range(2):
+                    for g in range(PASSES):
+                        mm_pass(u, hh, g)
+
+        def prod(u):
+            for hh in range(2):
+                h = 2 * u + hh
+                a1 = work.tile([P, 512], F32, tag="a1", name="a1_%d" % h, bufs=4)
+                a2 = work.tile([P, 512], F32, tag="a2", name="a2_%d" % h, bufs=4)
+                prod_t[h] = (a1, a2)
+                nc.vector.scalar_tensor_tensor(out=a1[:], in0=zt[(u, hh)][:], scalar=bias[:, h : h + 1],
+                                               in1=cos_t[:], op0=ALU.add, op1=ALU.mult)
+                nc.vector.scalar_tensor_tensor(out=a2[:], in0=zt[(u, hh)][:], scalar=bias[:, h : h + 1],
+                                               in1=sin_t[:], op0=ALU.add, op1=ALU.mult)
+
+        def back(u):
+            for hh in range(2):
+                h = 2 * u + hh
+                o = psum.tile([P, 512], F32, tag="t", name="o%d" % h)
+                ot[h] = o
+                a1, a2 = prod_t[h]
+                for a in range(4):
+                    cols = slice(P * a, P * (a + 1))
+                    nc.tensor.matmul(out=o[:, cols], lhsT=a1[:, cols], rhs=ident[:], start=True, stop=False,
+                                     is_transpose=True)
+                    nc.tensor.matmul(out=o[:, cols], lhsT=a2[:, cols], rhs=swap[:], start=False, stop=True,
+                                     is_transpose=True)
+
+        def evac(u):
+            for hh in range(2):
+                h = 2 * u + hh
+                nc.scalar.copy(out=out_sb[:, 512 * h : 512 * (h + 1)], in_=ot[h][:])
+
+        def store(u):
+            nc.sync.dma_start(
+                out=o0v[:, 2 * u : 2 * u + 2, :],
+                in_=out_sb[:, 1024 * u : 1024 * (u + 1)].rearrange("p (h f) -> p h f", h=2),
+            )
+
+        def absmax(col, lo, hi):
+            nc.vector.tensor_reduce(out=pm[:, col : col + 1], in_=out_sb[:, lo:hi], axis=AX.X, op=ALU.max,
+                                    apply_absolute_value=True)
+
+        def x_transposes(g):
+            for ap in range(2):
+                t = psum.tile([P, 512], F32, tag=("t" if g < 2 else "z"), name="xt%d_%d" % (g, ap))
+                xt[(g, ap)] = t
+                for a2 in range(2):
+                    words = xs[g][:, 2 * ap + a2, :].bitcast(F32)
+                    for uu in range(2):
+                        k = 2 * a2 + uu
+                        nc.tensor.transpose(out=t[:, P * k : P * (k + 1)], in_=words[:, uu:256:2], identity=ident[:])
+
+        def x_evac(eng, g, ap):
+            if ap == 0:
+                xg[g] = work.tile([P, 2048], BF16, tag="xg", name="xg%d" % g, bufs=2, align_bytes=64)
+            dst = xg[g][:].bitcast(F32).rearrange("p (a r u) -> p a r u", a=4, u=2)[:, 2 * ap : 2 * ap + 2]
+            src = xt[(g, ap)][:].rearrange("p (a u r) -> p a r u", a=2, u=2)
+            if eng == "S":
+                nc.scalar.copy(out=dst, in_=src)
+            else:
+                nc.vector.tensor_copy(out=dst, in_=src)
+
+        def x_quant(g):
+            xq[g] = const.tile([P, 512], U32, name="xq%d" % g, align_bytes=64)
+            xsc[g] = const.tile([P, 512], U8, name="xsc%d" % g, align_bytes=64)
+            nc.vector.quantize_mx(out=xq[g][:].bitcast(FP8X4), scales=xsc[g][:], in_=xg[g][:])
+
+        interleave("S", 0, 0)
+        interleave("G", 0, 1)
+
+        tv = const.tile([P, 512], F32, name="tv")
+        tk = const.tile([P, 512], I32, name="tk")
+        tf = const.tile([P, 512], F32, name="tf")
+        tn = const.tile([P, 512], F32, name="tn")
+        ts = const.tile([P, 512], F32, name="ts")
+        th = const.tile([P, 512], F32, name="th")
+        tcn = const.tile([P, 512], F32, name="tcn")
+        nc.vector.tensor_scalar(out=tv[:], in0=m_idx[:], scalar1=ucol[:, 0:1], scalar2=None, op0=ALU.mult)
+        nc.vector.tensor_copy(out=tk[:], in_=tv[:])
+        nc.vector.tensor_tensor(out=tf[:], in0=tv[:], in1=tk[:], op=ALU.subtract)
+        nc.vector.scalar_tensor_tensor(out=tn[:], in0=tf[:], scalar=0.5, in1=tf[:], op0=ALU.is_gt, op1=ALU.subtract)
+        nc.vector.tensor_scalar(out=ts[:], in0=tn[:], scalar1=sgn[:, 0:1], scalar2=None, op0=ALU.mult)
+        nc.vector.tensor_scalar(out=th[:], in0=tn[:], scalar1=-1.0, scalar2=0.25, op0=ALU.mult, op1=ALU.add)
+        nc.vector.scalar_tensor_tensor(out=tcn[:], in0=th[:], scalar=0.5, in1=th[:], op0=ALU.is_gt, op1=ALU.subtract)
+        nc.scalar.activation(out=sin_t[:], in_=ts[:], func=ACT.Sin, scale=-TWO_PI)
+        nc.scalar.activation(out=cos_t[:], in_=tcn[:], func=ACT.Sin, scale=-TWO_PI)
+
+        quant(0)
+        x_transposes(0)
+        x_transposes(1)
+        x_transposes(2)
+        x_transposes(3)
+        for g in range(PASSES):
+            x_evac("S", g, 0)
+            x_evac("S" if g < 3 else "V", g, 1)
+            x_quant(g)
+        interleave("S", 1, 0)
+        interleave("G", 1, 1)
+        mm(0, True)
+
+        for i in range(UNITS):
+            if i + 2 < UNITS:
+                interleave("S", i + 2, 0)
+            if i + 1 < UNITS:
+                quant(i + 1)
+            if i + 2 < UNITS:
+                interleave("G", i + 2, 1)
+            if i + 1 < UNITS:
+                mm(i + 1, False)
+            prod(i)
+            back(i)
+            evac(i)
+            store(i)
+            if i >= 1:
+                absmax(i - 1, 1024 * (i - 1), 1024 * i)
+        absmax(7, 1024 * 7, 1024 * 7 + 512)
+        absmax(8, 1024 * 7 + 512, 1024 * 8)
+
+        nc.vector.tensor_reduce(out=pmax[:], in_=pm[:, 0:9], axis=AX.X, op=ALU.max)
+        pa = psum.tile([P, 512], F32, tag="t", name="pa")
+        nc.tensor.transpose(out=pa[:, 0:P], in_=pmax[:, 0:1].to_broadcast([P, P]), identity=ident[:])
+        nc.vector.tensor_reduce(out=amax[:], in_=pa[:, 0:P], axis=AX.X, op=ALU.max)
+        nc.vector.reciprocal(out=rec[:], in_=amax[:])
+        nc.vector.tensor_scalar(out=fac[:], in0=rec[:], scalar1=448.0, scalar2=None, op0=ALU.mult)
+        for d in range(4):
+            lo = 2048 * d
+            mid = lo + V_SHARE
+            hi = lo + 2048
+            nc.vector.tensor_scalar(out=o8[:, lo:mid], in0=out_sb[:, lo:mid], scalar1=fac[:, 0:1], scalar2=None,
+                                    op0=ALU.mult, saturate=False)
+            nc.scalar.activation(out=o8[:, mid:hi], in_=out_sb[:, mid:hi], func=ACT.Identity, scale=fac[:, 0:1],
+                                 bias=zero[:, 0:1], saturate=False)
+            nc.sync.dma_start(
+                out=o1v[:, 4 * d : 4 * d + 4, :],
+                in_=o8[:, lo:hi].bitcast(U8).rearrange("p (h f) -> p h f", h=4),
+            )

@@ -19,8 +19,10 @@ AX = mybir.AxisListType
 P = 128
 PASSES = 4
 UNITS = 8
-W_RANGES = ((0, 256), (256, 256), (512, 512), (1024, 512), (1536, 512))
-V_SHARE = 1344
+HEADS = 16
+W_RANGES = ((0, 256), (256, 256), (512, 256), (768, 256), (1024, 512), (1536, 512))
+V_SHARE = 336
+CAST_GROUPS = ((0, 2), (2, 2), (4, 4), (8, 4), (12, 4))
 TWO_PI = 6.283185307179586
 
 
@@ -36,66 +38,73 @@ def tile_multiheadedattention_pa_kernel(tc, x, w, b, out_0, out_1):
         o0v = out_0[0].rearrange("h (r a) j -> r h (a j)", a=4)
         o1v = out_1[0].rearrange("h (r a) j -> r h (a j)", a=4)
 
-        b16 = const.tile([16, P], BF16, name="b16")
-        nc.sync.dma_start(out=b16[:], in_=b.rearrange("(h c) -> h c", c=P))
         wraw = {}
         xs = {}
 
-        def load_w(c0, width):
-            for g in range(PASSES):
-                t = const.tile([P, 4, width], BF16, name="wr%d_%d" % (c0, g))
-                nc.sync.dma_start(
-                    out=t[:],
-                    in_=w[512 * g : 512 * (g + 1), c0 : c0 + width].rearrange("(p j) n -> p j n", j=4),
-                )
-                wraw[(c0, g)] = t
+        def load_w(c0, width, g):
+            t = const.tile([P, 4, width], BF16, name="wr%d_%d" % (c0, g))
+            nc.sync.dma_start(
+                out=t[:],
+                in_=w[512 * g : 512 * (g + 1), c0 : c0 + width].rearrange("(p j) n -> p j n", j=4),
+            )
+            wraw[(c0, g)] = t
 
-        load_w(W_RANGES[0][0], W_RANGES[0][1])
-        for g in range(PASSES):
-            t = const.tile([P, 4, 512], BF16, name="xs%d" % g)
-            nc.sync.dma_start(out=t[:], in_=xv[:, :, 512 * g : 512 * (g + 1)])
-            xs[g] = t
+        def load_x(a):
+            t = const.tile([P, 2048], BF16, name="xs%d" % a)
+            nc.sync.dma_start(out=t[:], in_=xv[:, a, :])
+            xs[a] = t
+
+        b16 = const.tile([16, P], BF16, name="b16")
+        nc.sync.dma_start(out=b16[:], in_=b.rearrange("(h c) -> h c", c=P))
+        load_x(0)
+        load_x(1)
+        load_w(0, 256, 0)
+        load_w(0, 256, 1)
+        load_x(2)
+        load_x(3)
+        load_w(0, 256, 2)
+        load_w(0, 256, 3)
         for c0, width in W_RANGES[1:]:
-            load_w(c0, width)
+            for g in range(PASSES):
+                load_w(c0, width, g)
 
-        def raw(u, g):
+        def raw(u, g, lo, hi):
             col = 256 * u
             for c0, width in W_RANGES:
                 if c0 <= col < c0 + width:
-                    return wraw[(c0, g)][:, :, col - c0 : col - c0 + 256]
+                    return wraw[(c0, g)][:, :, col - c0 + lo : col - c0 + hi]
             return None
 
         ident = const.tile([P, P], F32, name="ident")
         swap = const.tile([P, P], F32, name="swap")
         m_idx = const.tile([P, 512], I32, name="m_idx")
-        p_idx = const.tile([P, 1], I32, name="p_idx")
-        par = const.tile([P, 1], I32, name="par")
-        sgn = const.tile([P, 1], F32, name="sgn")
         zero = const.tile([P, 1], F32, name="zero")
         warm = const.tile([P, 1], F32, name="warm")
         freq = const.tile([P, P], F32, name="freq")
         turns = const.tile([P, P], F32, name="turns")
         b32 = const.tile([P, P], F32, name="b32")
         ucol = const.tile([P, 1], F32, name="ucol")
-        bias = const.tile([P, 16], F32, name="bias")
+        bias = const.tile([P, HEADS], F32, name="bias")
+        tk = const.tile([P, 512], I32, name="tk")
+        tg = const.tile([P, 512], F32, name="tg")
+        ta = const.tile([P, 512], F32, name="ta")
         cos_t = const.tile([P, 512], F32, name="cos_t")
         sin_t = const.tile([P, 512], F32, name="sin_t")
-        out_sb = const.tile([P, 16 * 512], F32, name="out_sb")
-        o8 = const.tile([P, 16 * 512], FP8, name="o8")
-        pm = const.tile([P, 16], F32, name="pm")
+        out_sb = const.tile([P, HEADS * 512 + 16], F32, name="out_sb")
+        o8 = const.tile([P, HEADS * 512], FP8, name="o8")
         pmax = const.tile([P, 1], F32, name="pmax")
-        amax = const.tile([P, 1], F32, name="amax")
-        rec = const.tile([P, 1], F32, name="rec")
+        junk = const.tile([P, P], F32, name="junk")
+        scl = const.tile([P, 1], F32, name="scl")
         fac = const.tile([P, 1], F32, name="fac")
+        PM0 = HEADS * 512
 
         make_identity(nc, ident[:])
         nc.gpsimd.iota(m_idx[:], pattern=[[1, 4], [4, P]], base=0, channel_multiplier=0)
-        nc.gpsimd.iota(p_idx[:], pattern=[[0, 1]], base=0, channel_multiplier=1)
 
         nc.vector.memset(zero[:], 0.0)
         nc.scalar.activation(out=warm[:], in_=zero[:], func=ACT.Sin)
-        nc.vector.memset(freq[:, 0:2], 1.0)
-        nc.vector.memset(b32[:], 0.0)
+        nc.vector.memset(freq[:, 0:1], 1.0)
+        nc.vector.memset(freq[:, 1:2], -1.0)
         for s in range(6):
             n = 2 << s
             nc.vector.tensor_scalar(
@@ -103,18 +112,24 @@ def tile_multiheadedattention_pa_kernel(tc, x, w, b, out_0, out_1):
                 scalar1=10000.0 ** (-(n // 2) / 64.0), scalar2=None, op0=ALU.mult,
             )
         nc.vector.tensor_scalar(out=turns[:], in0=freq[:], scalar1=1.0 / TWO_PI, scalar2=None, op0=ALU.mult)
-        nc.vector.tensor_copy(out=b32[0:16, :], in_=b16[:])
         pc = psum.tile([P, 512], F32, tag="t", name="pc")
         nc.tensor.transpose(out=pc[:, 0:P], in_=turns[:], identity=ident[:])
-        nc.tensor.transpose(out=pc[:, P : 2 * P], in_=b32[:], identity=ident[:])
-        nc.vector.tensor_copy(out=ucol[:], in_=pc[:, 0:1])
-        nc.vector.tensor_copy(out=bias[:], in_=pc[:, P : P + 16])
+        nc.vector.memset(b32[:], 0.0)
         idv = ident[:].rearrange("p (i e) -> p i e", e=2)
         swv = swap[:].rearrange("p (i e) -> p i e", e=2)
         nc.vector.tensor_copy(out=swv[:, :, 0:1], in_=idv[:, :, 1:2])
         nc.vector.tensor_copy(out=swv[:, :, 1:2], in_=idv[:, :, 0:1])
-        nc.vector.tensor_scalar(out=par[:], in0=p_idx[:], scalar1=1, scalar2=None, op0=ALU.bitwise_and)
-        nc.vector.tensor_scalar(out=sgn[:], in0=par[:], scalar1=-2.0, scalar2=1.0, op0=ALU.mult, op1=ALU.add)
+        nc.vector.tensor_copy(out=ucol[:], in_=pc[:, 0:1])
+        nc.vector.tensor_scalar(out=tk[:], in0=m_idx[:], scalar1=ucol[:, 0:1], scalar2=None, op0=ALU.mult)
+        nc.vector.scalar_tensor_tensor(out=tg[:], in0=m_idx[:], scalar=ucol[:, 0:1], in1=tk[:],
+                                       op0=ALU.mult, op1=ALU.subtract)
+        nc.scalar.activation(out=sin_t[:], in_=tg[:], func=ACT.Sin, scale=TWO_PI)
+        nc.vector.scalar_tensor_tensor(out=ta[:], in0=tg[:], scalar=-1.0, in1=tg[:], op0=ALU.mult, op1=ALU.max)
+        nc.scalar.activation(out=cos_t[:], in_=ta[:], func=ACT.Sin, scale=-TWO_PI, bias=TWO_PI / 4.0)
+        nc.vector.tensor_copy(out=b32[0:16, :], in_=b16[:])
+        pc2 = psum.tile([P, 512], F32, tag="z", name="pc2")
+        nc.tensor.transpose(out=pc2[:, 0:P], in_=b32[:], identity=ident[:])
+        nc.vector.tensor_copy(out=bias[:], in_=pc2[:, 0:HEADS])
 
         wg = {}
         wq = {}
@@ -127,35 +142,38 @@ def tile_multiheadedattention_pa_kernel(tc, x, w, b, out_0, out_1):
         xq = {}
         xsc = {}
 
-        def interleave(eng, u, half):
-            t = work.tile([P, 2, 256, 4], BF16, tag="wg%d" % half, name="wg%d_%d" % (half, u),
-                          bufs=(2 if half == 0 else 1), align_bytes=64)
-            wg[(u, half)] = t
-            for gg in range(2):
-                src = raw(u, 2 * half + gg).rearrange("p j c -> p c j")
-                dst = t[:, gg, :, :]
-                if eng == "S":
-                    nc.scalar.copy(out=dst, in_=src)
-                elif eng == "G":
-                    nc.gpsimd.tensor_scalar(out=dst, in0=src, scalar1=1.0, scalar2=0.0, op0=ALU.mult, op1=ALU.add)
-                else:
-                    nc.vector.tensor_copy(out=dst, in_=src)
+        def il(eng, u, g, lo, hi):
+            half = g // 2
+            if (u, half) not in wg:
+                wg[(u, half)] = work.tile([P, 2, 256, 4], BF16, tag="wg%d" % half, name="wg%d_%d" % (half, u),
+                                          bufs=(2 if half == 0 else 1), align_bytes=64)
+            src = raw(u, g, lo, hi).rearrange("p j c -> p c j")
+            dst = wg[(u, half)][:, g % 2, lo:hi, :]
+            if eng == "S":
+                nc.scalar.copy(out=dst, in_=src)
+            elif eng == "G":
+                nc.gpsimd.tensor_scalar(out=dst, in0=src, scalar1=1.0, scalar2=0.0, op0=ALU.mult, op1=ALU.add)
+            else:
+                nc.vector.tensor_copy(out=dst, in_=src)
 
-        def quant(u):
-            q = work.tile([P, PASSES, 256], U32, tag="wq", name="wq%d" % u, bufs=3, align_bytes=64)
-            s = work.tile([P, PASSES, 256], U8, tag="wsc", name="wsc%d" % u, bufs=3, align_bytes=64)
-            wq[u] = q
-            wsc[u] = s
-            for half in range(2):
-                nc.vector.quantize_mx(
-                    out=q[:, 2 * half : 2 * half + 2, :].rearrange("p g c -> p (g c)").bitcast(FP8X4),
-                    scales=s[:, 2 * half : 2 * half + 2, :].rearrange("p g c -> p (g c)"),
-                    in_=wg[(u, half)][:].rearrange("p g c j -> p (g c j)"),
-                )
+        def quant(u, half):
+            if half == 0:
+                wq[u] = work.tile([P, PASSES, 256], U32, tag="wq", name="wq%d" % u, bufs=3, align_bytes=64)
+                wsc[u] = work.tile([P, PASSES, 256], U8, tag="wsc", name="wsc%d" % u, bufs=3, align_bytes=64)
+            nc.vector.quantize_mx(
+                out=wq[u][:, 2 * half : 2 * half + 2, :].rearrange("p g c -> p (g c)").bitcast(FP8X4),
+                scales=wsc[u][:, 2 * half : 2 * half + 2, :].rearrange("p g c -> p (g c)"),
+                in_=wg[(u, half)][:].rearrange("p g c j -> p (g c j)"),
+            )
 
-        def mm_pass(u, hh, g):
+        def mm_open(h):
+            zt[h] = psum.tile([P, 512], F32, tag="z", name="z%d" % h)
+
+        def mm_pass(h, g):
+            u = h // 2
+            hh = h % 2
             nc.tensor.matmul_mx(
-                out=zt[(u, hh)][:],
+                out=zt[h][:],
                 lhsT=wq[u][:, g, P * hh : P * (hh + 1)].bitcast(FP8X4),
                 lhsT_scale=wsc[u][:, g, P * hh : P * (hh + 1)],
                 rhs=xq[g][:].bitcast(FP8X4),
@@ -164,46 +182,34 @@ def tile_multiheadedattention_pa_kernel(tc, x, w, b, out_0, out_1):
                 stop=(g == PASSES - 1),
             )
 
-        def mm(u, g_outer):
-            for hh in range(2):
-                zt[(u, hh)] = psum.tile([P, 512], F32, tag="z", name="z%d_%d" % (u, hh))
-            if g_outer:
-                for g in range(PASSES):
-                    for hh in range(2):
-                        mm_pass(u, hh, g)
-            else:
-                for hh in range(2):
-                    for g in range(PASSES):
-                        mm_pass(u, hh, g)
+        def mm(h):
+            mm_open(h)
+            for g in range(PASSES):
+                mm_pass(h, g)
 
-        def prod(u):
-            for hh in range(2):
-                h = 2 * u + hh
+        def prod(h, lo=0, hi=512):
+            if lo == 0:
                 a1 = work.tile([P, 512], F32, tag="a1", name="a1_%d" % h, bufs=4)
                 a2 = work.tile([P, 512], F32, tag="a2", name="a2_%d" % h, bufs=4)
                 prod_t[h] = (a1, a2)
-                nc.vector.scalar_tensor_tensor(out=a1[:], in0=zt[(u, hh)][:], scalar=bias[:, h : h + 1],
-                                               in1=cos_t[:], op0=ALU.add, op1=ALU.mult)
-                nc.vector.scalar_tensor_tensor(out=a2[:], in0=zt[(u, hh)][:], scalar=bias[:, h : h + 1],
-                                               in1=sin_t[:], op0=ALU.add, op1=ALU.mult)
+            a1, a2 = prod_t[h]
+            nc.vector.scalar_tensor_tensor(out=a1[:, lo:hi], in0=zt[h][:, lo:hi], scalar=bias[:, h : h + 1],
+                                           in1=cos_t[:, lo:hi], op0=ALU.add, op1=ALU.mult)
+            nc.vector.scalar_tensor_tensor(out=a2[:, lo:hi], in0=zt[h][:, lo:hi], scalar=bias[:, h : h + 1],
+                                           in1=sin_t[:, lo:hi], op0=ALU.add, op1=ALU.mult)
 
-        def back(u):
-            for hh in range(2):
-                h = 2 * u + hh
-                o = psum.tile([P, 512], F32, tag="t", name="o%d" % h)
-                ot[h] = o
-                a1, a2 = prod_t[h]
-                for a in range(4):
-                    cols = slice(P * a, P * (a + 1))
-                    nc.tensor.matmul(out=o[:, cols], lhsT=a1[:, cols], rhs=ident[:], start=True, stop=False,
-                                     is_transpose=True)
-                    nc.tensor.matmul(out=o[:, cols], lhsT=a2[:, cols], rhs=swap[:], start=False, stop=True,
-                                     is_transpose=True)
+        def back(h, lo=0, hi=512):
+            o = psum.tile([P, 512], F32, tag="t", name="o%d_%d" % (h, lo))
+            ot[(h, lo)] = o
+            a1, a2 = prod_t[h]
+            for c in range(lo, hi, P):
+                nc.tensor.matmul(out=o[:, c - lo : c - lo + P], lhsT=a1[:, c : c + P], rhs=ident[:], start=True,
+                                 stop=False, is_transpose=True)
+                nc.tensor.matmul(out=o[:, c - lo : c - lo + P], lhsT=a2[:, c : c + P], rhs=swap[:], start=False,
+                                 stop=True, is_transpose=True)
 
-        def evac(u):
-            for hh in range(2):
-                h = 2 * u + hh
-                nc.scalar.copy(out=out_sb[:, 512 * h : 512 * (h + 1)], in_=ot[h][:])
+        def evac(h, lo=0, hi=512):
+            nc.scalar.copy(out=out_sb[:, 512 * h + lo : 512 * h + hi], in_=ot[(h, lo)][:, 0 : hi - lo])
 
         def store(u):
             nc.sync.dma_start(
@@ -211,101 +217,140 @@ def tile_multiheadedattention_pa_kernel(tc, x, w, b, out_0, out_1):
                 in_=out_sb[:, 1024 * u : 1024 * (u + 1)].rearrange("p (h f) -> p h f", h=2),
             )
 
-        def absmax(col, lo, hi):
-            nc.vector.tensor_reduce(out=pm[:, col : col + 1], in_=out_sb[:, lo:hi], axis=AX.X, op=ALU.max,
+        def absmax(dst, lo, hi):
+            nc.vector.tensor_reduce(out=dst, in_=out_sb[:, lo:hi], axis=AX.X, op=ALU.max,
                                     apply_absolute_value=True)
 
-        def x_transposes(g):
-            for ap in range(2):
-                t = psum.tile([P, 512], F32, tag=("t" if g < 2 else "z"), name="xt%d_%d" % (g, ap))
-                xt[(g, ap)] = t
-                for a2 in range(2):
-                    words = xs[g][:, 2 * ap + a2, :].bitcast(F32)
-                    for uu in range(2):
-                        k = 2 * a2 + uu
-                        nc.tensor.transpose(out=t[:, P * k : P * (k + 1)], in_=words[:, uu:256:2], identity=ident[:])
+        def x_transposes(a, g):
+            ap = a // 2
+            a2 = a % 2
+            if a2 == 0:
+                xt[(g, ap)] = psum.tile([P, 512], F32, tag="t", name="xt%d_%d" % (g, ap))
+            words = xs[a][:, 512 * g : 512 * (g + 1)].bitcast(F32)
+            for uu in range(2):
+                k = 2 * a2 + uu
+                nc.tensor.transpose(out=xt[(g, ap)][:, P * k : P * (k + 1)], in_=words[:, uu:256:2],
+                                    identity=ident[:])
 
-        def x_evac(eng, g, ap):
-            if ap == 0:
-                xg[g] = work.tile([P, 2048], BF16, tag="xg", name="xg%d" % g, bufs=2, align_bytes=64)
-            dst = xg[g][:].bitcast(F32).rearrange("p (a r u) -> p a r u", a=4, u=2)[:, 2 * ap : 2 * ap + 2]
+        def x_evac(g, ap):
+            xg[(g, ap)] = work.tile([P, 1024], BF16, tag="xg", name="xg%d_%d" % (g, ap), bufs=3, align_bytes=64)
+            dst = xg[(g, ap)][:].bitcast(F32).rearrange("p (a r u) -> p a r u", a=2, u=2)
             src = xt[(g, ap)][:].rearrange("p (a u r) -> p a r u", a=2, u=2)
-            if eng == "S":
-                nc.scalar.copy(out=dst, in_=src)
-            else:
-                nc.vector.tensor_copy(out=dst, in_=src)
+            nc.scalar.copy(out=dst, in_=src)
 
-        def x_quant(g):
-            xq[g] = const.tile([P, 512], U32, name="xq%d" % g, align_bytes=64)
-            xsc[g] = const.tile([P, 512], U8, name="xsc%d" % g, align_bytes=64)
-            nc.vector.quantize_mx(out=xq[g][:].bitcast(FP8X4), scales=xsc[g][:], in_=xg[g][:])
+        def x_quant(g, ap):
+            if ap == 0:
+                xq[g] = const.tile([P, 512], U32, name="xq%d" % g, align_bytes=64)
+                xsc[g] = const.tile([P, 512], U8, name="xsc%d" % g, align_bytes=64)
+            nc.vector.quantize_mx(out=xq[g][:, 256 * ap : 256 * (ap + 1)].bitcast(FP8X4),
+                                  scales=xsc[g][:, 256 * ap : 256 * (ap + 1)], in_=xg[(g, ap)][:])
 
-        interleave("S", 0, 0)
-        interleave("G", 0, 1)
+        def dummies(n, name):
+            d = psum.tile([P, 512], F32, tag="z", name=name)
+            for k in range(n):
+                nc.tensor.matmul(out=d[:, 0:P], lhsT=ident[:], rhs=ident[:], start=True, stop=True)
 
-        tv = const.tile([P, 512], F32, name="tv")
-        tk = const.tile([P, 512], I32, name="tk")
-        tf = const.tile([P, 512], F32, name="tf")
-        tn = const.tile([P, 512], F32, name="tn")
-        ts = const.tile([P, 512], F32, name="ts")
-        th = const.tile([P, 512], F32, name="th")
-        tcn = const.tile([P, 512], F32, name="tcn")
-        nc.vector.tensor_scalar(out=tv[:], in0=m_idx[:], scalar1=ucol[:, 0:1], scalar2=None, op0=ALU.mult)
-        nc.vector.tensor_copy(out=tk[:], in_=tv[:])
-        nc.vector.tensor_tensor(out=tf[:], in0=tv[:], in1=tk[:], op=ALU.subtract)
-        nc.vector.scalar_tensor_tensor(out=tn[:], in0=tf[:], scalar=0.5, in1=tf[:], op0=ALU.is_gt, op1=ALU.subtract)
-        nc.vector.tensor_scalar(out=ts[:], in0=tn[:], scalar1=sgn[:, 0:1], scalar2=None, op0=ALU.mult)
-        nc.vector.tensor_scalar(out=th[:], in0=tn[:], scalar1=-1.0, scalar2=0.25, op0=ALU.mult, op1=ALU.add)
-        nc.vector.scalar_tensor_tensor(out=tcn[:], in0=th[:], scalar=0.5, in1=th[:], op0=ALU.is_gt, op1=ALU.subtract)
-        nc.scalar.activation(out=sin_t[:], in_=ts[:], func=ACT.Sin, scale=-TWO_PI)
-        nc.scalar.activation(out=cos_t[:], in_=tcn[:], func=ACT.Sin, scale=-TWO_PI)
-
-        quant(0)
-        x_transposes(0)
-        x_transposes(1)
-        x_transposes(2)
-        x_transposes(3)
-        for g in range(PASSES):
-            x_evac("S", g, 0)
-            x_evac("S" if g < 3 else "V", g, 1)
-            x_quant(g)
-        interleave("S", 1, 0)
-        interleave("G", 1, 1)
-        mm(0, True)
+        for a in range(2):
+            for g in range(PASSES):
+                x_transposes(a, g)
+        il("V", 0, 0, 0, 256)
+        x_evac(0, 0)
+        x_quant(0, 0)
+        x_evac(1, 0)
+        x_quant(1, 0)
+        il("V", 0, 1, 0, 256)
+        x_evac(2, 0)
+        x_quant(2, 0)
+        x_evac(3, 0)
+        x_quant(3, 0)
+        quant(0, 0)
+        for a in range(2, 4):
+            for g in range(PASSES):
+                x_transposes(a, g)
+        dummies(3, "dz0")
+        mm_open(0)
+        mm_open(1)
+        x_evac(0, 1)
+        il("V", 0, 2, 0, 256)
+        x_quant(0, 1)
+        mm_pass(0, 0)
+        mm_pass(1, 0)
+        x_evac(1, 1)
+        il("V", 0, 3, 0, 256)
+        x_quant(1, 1)
+        mm_pass(0, 1)
+        mm_pass(1, 1)
+        x_evac(2, 1)
+        x_quant(2, 1)
+        x_evac(3, 1)
+        x_quant(3, 1)
+        quant(0, 1)
+        mm_pass(0, 2)
+        mm_pass(0, 3)
+        mm_pass(1, 2)
+        mm_pass(1, 3)
+        il("G", 1, 2, 128, 256)
+        il("G", 1, 3, 0, 256)
+        il("S", 1, 0, 0, 256)
+        il("S", 1, 1, 0, 256)
+        il("S", 1, 2, 0, 128)
 
         for i in range(UNITS):
-            if i + 2 < UNITS:
-                interleave("S", i + 2, 0)
-            if i + 1 < UNITS:
-                quant(i + 1)
-            if i + 2 < UNITS:
-                interleave("G", i + 2, 1)
-            if i + 1 < UNITS:
-                mm(i + 1, False)
-            prod(i)
-            back(i)
-            evac(i)
-            store(i)
+            prod(2 * i)
+            back(2 * i)
             if i >= 1:
-                absmax(i - 1, 1024 * (i - 1), 1024 * i)
-        absmax(7, 1024 * 7, 1024 * 7 + 512)
-        absmax(8, 1024 * 7 + 512, 1024 * 8)
+                evac(2 * i - 1)
+                store(i - 1)
+            if i + 2 < UNITS:
+                il("S", i + 2, 0, 0, 256)
+            if i == 1:
+                absmax(out_sb[:, PM0 : PM0 + 1], 0, 512)
+            if i >= 2:
+                absmax(out_sb[:, PM0 + i - 1 : PM0 + i], 512 * (2 * i - 3), 512 * (2 * i - 1))
+            evac(2 * i)
+            if i + 1 < UNITS:
+                quant(i + 1, 0)
+                quant(i + 1, 1)
+            if i + 2 < UNITS:
+                il("S", i + 2, 2, 0, 128)
+                il("G", i + 2, 2, 128, 256)
+                il("G", i + 2, 3, 0, 256)
+            if i + 1 < UNITS:
+                mm(2 * i + 2)
+            else:
+                dummies(3, "dz1")
+            if i + 2 < UNITS:
+                il("S", i + 2, 1, 0, 256)
+            if i + 1 < UNITS:
+                prod(2 * i + 1)
+                back(2 * i + 1)
+                mm(2 * i + 3)
+        prod(15, 0, 256)
+        back(15, 0, 256)
+        prod(15, 256, 512)
+        back(15, 256, 512)
+        evac(15, 0, 256)
+        evac(15, 256, 512)
+        store(7)
+        absmax(out_sb[:, PM0 + 7 : PM0 + 8], 512 * 13, 512 * 14)
+        absmax(out_sb[:, PM0 + 8 : PM0 + 9], 512 * 14, 512 * 15)
+        absmax(out_sb[:, PM0 + 9 : PM0 + 10], 512 * 15, 512 * 15 + 256)
+        absmax(pmax[:], 512 * 15 + 256, PM0 + 10)
 
-        nc.vector.tensor_reduce(out=pmax[:], in_=pm[:, 0:9], axis=AX.X, op=ALU.max)
         pa = psum.tile([P, 512], F32, tag="t", name="pa")
         nc.tensor.transpose(out=pa[:, 0:P], in_=pmax[:, 0:1].to_broadcast([P, P]), identity=ident[:])
-        nc.vector.tensor_reduce(out=amax[:], in_=pa[:, 0:P], axis=AX.X, op=ALU.max)
-        nc.vector.reciprocal(out=rec[:], in_=amax[:])
-        nc.vector.tensor_scalar(out=fac[:], in0=rec[:], scalar1=448.0, scalar2=None, op0=ALU.mult)
-        for d in range(4):
-            lo = 2048 * d
-            mid = lo + V_SHARE
-            hi = lo + 2048
+        nc.vector.tensor_scalar(out=junk[:], in0=pa[:, 0:P], scalar1=1.0 / 448.0, scalar2=None, op0=ALU.mult,
+                                op1=ALU.max, accum_out=scl[:, 0:1])
+        nc.vector.reciprocal(out=fac[:], in_=scl[:])
+        for h0, nh in CAST_GROUPS:
+            lo = 512 * h0
+            mid = lo + V_SHARE * nh
+            hi = lo + 512 * nh
             nc.vector.tensor_scalar(out=o8[:, lo:mid], in0=out_sb[:, lo:mid], scalar1=fac[:, 0:1], scalar2=None,
                                     op0=ALU.mult, saturate=False)
             nc.scalar.activation(out=o8[:, mid:hi], in_=out_sb[:, mid:hi], func=ACT.Identity, scale=fac[:, 0:1],
                                  bias=zero[:, 0:1], saturate=False)
             nc.sync.dma_start(
-                out=o1v[:, 4 * d : 4 * d + 4, :],
-                in_=o8[:, lo:hi].bitcast(U8).rearrange("p (h f) -> p h f", h=4),
+                out=o1v[:, h0 : h0 + nh, :],
+                in_=o8[:, lo:hi].bitcast(U8).rearrange("p (h f) -> p h f", h=nh),
             )

@@ -88,8 +88,7 @@ def tile_multiheadedattention_pa_kernel(tc, x, w, b, out_0, out_1):
         tk = const.tile([P, 512], I32, name="tk")
         tg = const.tile([P, 512], F32, name="tg")
         ta = const.tile([P, 512], F32, name="ta")
-        cos_t = const.tile([P, 512], F32, name="cos_t")
-        sin_t = const.tile([P, 512], F32, name="sin_t")
+        tab = const.tile([P, 2, 512], F32, name="tab")
         out_sb = const.tile([P, HEADS * 512 + 16], F32, name="out_sb")
         o8 = const.tile([P, HEADS * 512], FP8, name="o8")
         pmax = const.tile([P, 1], F32, name="pmax")
@@ -123,13 +122,8 @@ def tile_multiheadedattention_pa_kernel(tc, x, w, b, out_0, out_1):
         nc.vector.tensor_scalar(out=tk[:], in0=m_idx[:], scalar1=ucol[:, 0:1], scalar2=None, op0=ALU.mult)
         nc.vector.scalar_tensor_tensor(out=tg[:], in0=m_idx[:], scalar=ucol[:, 0:1], in1=tk[:],
                                        op0=ALU.mult, op1=ALU.subtract)
-        nc.scalar.activation(out=sin_t[:], in_=tg[:], func=ACT.Sin, scale=TWO_PI)
         nc.vector.scalar_tensor_tensor(out=ta[:], in0=tg[:], scalar=-1.0, in1=tg[:], op0=ALU.mult, op1=ALU.max)
-        nc.scalar.activation(out=cos_t[:], in_=ta[:], func=ACT.Sin, scale=-TWO_PI, bias=TWO_PI / 4.0)
         nc.vector.tensor_copy(out=b32[0:16, :], in_=b16[:])
-        pc2 = psum.tile([P, 512], F32, tag="z", name="pc2")
-        nc.tensor.transpose(out=pc2[:, 0:P], in_=b32[:], identity=ident[:])
-        nc.vector.tensor_copy(out=bias[:], in_=pc2[:, 0:HEADS])
 
         wg = {}
         wq = {}
@@ -147,8 +141,12 @@ def tile_multiheadedattention_pa_kernel(tc, x, w, b, out_0, out_1):
             if (u, half) not in wg:
                 wg[(u, half)] = work.tile([P, 2, 256, 4], BF16, tag="wg%d" % half, name="wg%d_%d" % (half, u),
                                           bufs=(2 if half == 0 else 1), align_bytes=64)
-            src = raw(u, g, lo, hi).rearrange("p j c -> p c j")
-            dst = wg[(u, half)][:, g % 2, lo:hi, :]
+            if eng == "G":
+                src = raw(u, g, lo, hi).rearrange("p j c -> p c j")
+                dst = wg[(u, half)][:, g % 2, lo:hi, :]
+            else:
+                src = raw(u, g, lo, hi).rearrange("p j (c i) -> p c j i", i=4)
+                dst = wg[(u, half)][:, g % 2, lo:hi, :].rearrange("p (c i) j -> p c j i", i=4)
             if eng == "S":
                 nc.scalar.copy(out=dst, in_=src)
             elif eng == "G":
@@ -189,23 +187,24 @@ def tile_multiheadedattention_pa_kernel(tc, x, w, b, out_0, out_1):
 
         def prod(h, lo=0, hi=512):
             if lo == 0:
-                a1 = work.tile([P, 512], F32, tag="a1", name="a1_%d" % h, bufs=4)
-                a2 = work.tile([P, 512], F32, tag="a2", name="a2_%d" % h, bufs=4)
-                prod_t[h] = (a1, a2)
-            a1, a2 = prod_t[h]
-            nc.vector.scalar_tensor_tensor(out=a1[:, lo:hi], in0=zt[h][:, lo:hi], scalar=bias[:, h : h + 1],
-                                           in1=cos_t[:, lo:hi], op0=ALU.add, op1=ALU.mult)
-            nc.vector.scalar_tensor_tensor(out=a2[:, lo:hi], in0=zt[h][:, lo:hi], scalar=bias[:, h : h + 1],
-                                           in1=sin_t[:, lo:hi], op0=ALU.add, op1=ALU.mult)
+                prod_t[h] = work.tile([P, 2, 512], F32, tag="at", name="at_%d" % h, bufs=4)
+            nc.vector.scalar_tensor_tensor(
+                out=prod_t[h][:, :, lo:hi],
+                in0=zt[h][:, lo:hi].unsqueeze(1).to_broadcast([P, 2, hi - lo]),
+                scalar=bias[:, h : h + 1],
+                in1=tab[:, :, lo:hi],
+                op0=ALU.add,
+                op1=ALU.mult,
+            )
 
         def back(h, lo=0, hi=512):
             o = psum.tile([P, 512], F32, tag="t", name="o%d_%d" % (h, lo))
             ot[(h, lo)] = o
-            a1, a2 = prod_t[h]
+            at = prod_t[h]
             for c in range(lo, hi, P):
-                nc.tensor.matmul(out=o[:, c - lo : c - lo + P], lhsT=a1[:, c : c + P], rhs=ident[:], start=True,
+                nc.tensor.matmul(out=o[:, c - lo : c - lo + P], lhsT=at[:, 0, c : c + P], rhs=ident[:], start=True,
                                  stop=False, is_transpose=True)
-                nc.tensor.matmul(out=o[:, c - lo : c - lo + P], lhsT=a2[:, c : c + P], rhs=swap[:], start=False,
+                nc.tensor.matmul(out=o[:, c - lo : c - lo + P], lhsT=at[:, 1, c : c + P], rhs=swap[:], start=False,
                                  stop=True, is_transpose=True)
 
         def evac(h, lo=0, hi=512):
@@ -253,6 +252,8 @@ def tile_multiheadedattention_pa_kernel(tc, x, w, b, out_0, out_1):
         for a in range(2):
             for g in range(PASSES):
                 x_transposes(a, g)
+        pc2 = psum.tile([P, 512], F32, tag="z", name="pc2")
+        nc.tensor.transpose(out=pc2[:, 0:P], in_=b32[:], identity=ident[:])
         il("V", 0, 0, 0, 256)
         x_evac(0, 0)
         x_quant(0, 0)
@@ -270,6 +271,8 @@ def tile_multiheadedattention_pa_kernel(tc, x, w, b, out_0, out_1):
         dummies(3, "dz0")
         mm_open(0)
         mm_open(1)
+        nc.scalar.activation(out=tab[:, 1, :], in_=tg[:], func=ACT.Sin, scale=TWO_PI)
+        nc.scalar.activation(out=tab[:, 0, :], in_=ta[:], func=ACT.Sin, scale=-TWO_PI, bias=TWO_PI / 4.0)
         x_evac(0, 1)
         il("V", 0, 2, 0, 256)
         x_quant(0, 1)
@@ -284,6 +287,7 @@ def tile_multiheadedattention_pa_kernel(tc, x, w, b, out_0, out_1):
         x_quant(2, 1)
         x_evac(3, 1)
         x_quant(3, 1)
+        nc.vector.tensor_copy(out=bias[:], in_=pc2[:, 0:HEADS])
         quant(0, 1)
         mm_pass(0, 2)
         mm_pass(0, 3)

@@ -249,6 +249,19 @@ def tile_multiheadedattention_pa_kernel(tc, x, w, b, out_0, out_1):
             for k in range(n):
                 nc.tensor.matmul(out=d[:, 0:P], lhsT=ident[:], rhs=ident[:], start=True, stop=True)
 
+        zb = {}
+
+        def zbias(h, lo=0, hi=512):
+            zb[h] = work.tile([P, 512], F32, tag="zb", name="zb%d" % h, bufs=2)
+            nc.scalar.activation(out=zb[h][:, lo:hi], in_=zt[h][:, lo:hi], func=ACT.Identity, bias=bias[:, h : h + 1],
+                                 scale=1.0)
+
+        def gprod(h, lo, hi, fresh):
+            if fresh:
+                prod_t[h] = work.tile([P, 2, 512], F32, tag="at", name="at_%d" % h, bufs=4)
+            for k in range(2):
+                nc.gpsimd.tensor_tensor(out=prod_t[h][:, k, lo:hi], in0=zb[h][:, lo:hi], in1=tab[:, k, lo:hi], op=ALU.mult)
+
         for a in range(2):
             for g in range(PASSES):
                 x_transposes(a, g)
@@ -299,7 +312,7 @@ def tile_multiheadedattention_pa_kernel(tc, x, w, b, out_0, out_1):
         il("S", 1, 1, 0, 256)
         il("S", 1, 2, 0, 128)
 
-        for i in range(UNITS):
+        for i in range(6):
             prod(2 * i)
             back(2 * i)
             if i >= 1:
@@ -329,17 +342,41 @@ def tile_multiheadedattention_pa_kernel(tc, x, w, b, out_0, out_1):
                 prod(2 * i + 1)
                 back(2 * i + 1)
                 mm(2 * i + 3)
+        prod(12)
+        evac(11)
+        store(5)
+        quant(7, 0)
+        quant(7, 1)
+        zbias(13)
+        mm(14)
+        mm(15)
+        back(12)
+        gprod(13, 0, 256, True)
+        gprod(13, 256, 512, False)
+        absmax(out_sb[:, PM0 + 5 : PM0 + 6], 512 * 9, 512 * 11)
+        prod(14)
+        zbias(15, 256, 512)
+        evac(12)
+        absmax(out_sb[:, PM0 + 6 : PM0 + 7], 512 * 11, 512 * 12)
         prod(15, 0, 256)
+        gprod(15, 256, 512, False)
+        back(13, 0, 256)
+        back(14)
+        back(13, 256, 512)
+        evac(13, 0, 256)
+        absmax(out_sb[:, PM0 + 7 : PM0 + 8], 512 * 12, 512 * 13)
+        evac(14)
+        evac(13, 256, 512)
+        store(6)
         back(15, 0, 256)
-        prod(15, 256, 512)
-        back(15, 256, 512)
+        absmax(out_sb[:, PM0 + 8 : PM0 + 9], 512 * 14, 512 * 15)
         evac(15, 0, 256)
+        back(15, 256, 512)
+        absmax(out_sb[:, PM0 + 9 : PM0 + 10], 512 * 13, 512 * 14)
         evac(15, 256, 512)
         store(7)
-        absmax(out_sb[:, PM0 + 7 : PM0 + 8], 512 * 13, 512 * 14)
-        absmax(out_sb[:, PM0 + 8 : PM0 + 9], 512 * 14, 512 * 15)
-        absmax(out_sb[:, PM0 + 9 : PM0 + 10], 512 * 15, 512 * 15 + 256)
-        absmax(pmax[:], 512 * 15 + 256, PM0 + 10)
+        absmax(out_sb[:, PM0 + 10 : PM0 + 11], 512 * 15, 512 * 15 + 256)
+        absmax(pmax[:], 512 * 15 + 256, PM0 + 11)
 
         pa = psum.tile([P, 512], F32, tag="t", name="pa")
         nc.tensor.transpose(out=pa[:, 0:P], in_=pmax[:, 0:1].to_broadcast([P, P]), identity=ident[:])

@@ -313,35 +313,26 @@ def tile_multiheadedattention_pa_kernel(tc, x, w, b, out_0, out_1):
         il("S", 1, 2, 0, 128)
 
         for i in range(6):
+            if i >= 2:
+                absmax(out_sb[:, PM0 + i - 2 : PM0 + i - 1], 512 * (2 * i - 4), 512 * (2 * i - 2))
             prod(2 * i)
             back(2 * i)
             if i >= 1:
                 evac(2 * i - 1)
                 store(i - 1)
-            if i + 2 < UNITS:
-                il("S", i + 2, 0, 0, 256)
-            if i == 1:
-                absmax(out_sb[:, PM0 : PM0 + 1], 0, 512)
-            if i >= 2:
-                absmax(out_sb[:, PM0 + i - 1 : PM0 + i], 512 * (2 * i - 3), 512 * (2 * i - 1))
+            il("S", i + 2, 0, 0, 256)
+            quant(i + 1, 0)
+            quant(i + 1, 1)
+            il("G", i + 2, 2, 128, 256)
+            il("G", i + 2, 3, 0, 256)
+            mm(2 * i + 2)
+            il("S", i + 2, 1, 0, 256)
             evac(2 * i)
-            if i + 1 < UNITS:
-                quant(i + 1, 0)
-                quant(i + 1, 1)
-            if i + 2 < UNITS:
-                il("S", i + 2, 2, 0, 128)
-                il("G", i + 2, 2, 128, 256)
-                il("G", i + 2, 3, 0, 256)
-            if i + 1 < UNITS:
-                mm(2 * i + 2)
-            else:
-                dummies(3, "dz1")
-            if i + 2 < UNITS:
-                il("S", i + 2, 1, 0, 256)
-            if i + 1 < UNITS:
-                prod(2 * i + 1)
-                back(2 * i + 1)
-                mm(2 * i + 3)
+            il("S", i + 2, 2, 0, 128)
+            prod(2 * i + 1)
+            back(2 * i + 1)
+            mm(2 * i + 3)
+        absmax(out_sb[:, PM0 + 4 : PM0 + 5], 512 * 8, 512 * 10)
         prod(12)
         evac(11)
         store(5)
@@ -353,30 +344,29 @@ def tile_multiheadedattention_pa_kernel(tc, x, w, b, out_0, out_1):
         back(12)
         gprod(13, 0, 256, True)
         gprod(13, 256, 512, False)
-        absmax(out_sb[:, PM0 + 5 : PM0 + 6], 512 * 9, 512 * 11)
+        absmax(out_sb[:, PM0 + 5 : PM0 + 6], 512 * 10, 512 * 12)
         prod(14)
         zbias(15, 256, 512)
         evac(12)
-        absmax(out_sb[:, PM0 + 6 : PM0 + 7], 512 * 11, 512 * 12)
         prod(15, 0, 256)
         gprod(15, 256, 512, False)
         back(13, 0, 256)
         back(14)
         back(13, 256, 512)
         evac(13, 0, 256)
-        absmax(out_sb[:, PM0 + 7 : PM0 + 8], 512 * 12, 512 * 13)
+        absmax(out_sb[:, PM0 + 6 : PM0 + 7], 512 * 12, 512 * 13)
         evac(14)
         evac(13, 256, 512)
         store(6)
         back(15, 0, 256)
-        absmax(out_sb[:, PM0 + 8 : PM0 + 9], 512 * 14, 512 * 15)
+        absmax(out_sb[:, PM0 + 7 : PM0 + 8], 512 * 14, 512 * 15)
         evac(15, 0, 256)
         back(15, 256, 512)
-        absmax(out_sb[:, PM0 + 9 : PM0 + 10], 512 * 13, 512 * 14)
+        absmax(out_sb[:, PM0 + 8 : PM0 + 9], 512 * 13, 512 * 14)
         evac(15, 256, 512)
         store(7)
-        absmax(out_sb[:, PM0 + 10 : PM0 + 11], 512 * 15, 512 * 15 + 256)
-        absmax(pmax[:], 512 * 15 + 256, PM0 + 11)
+        absmax(out_sb[:, PM0 + 9 : PM0 + 10], 512 * 15, 512 * 15 + 256)
+        absmax(pmax[:], 512 * 15 + 256, PM0 + 10)
 
         pa = psum.tile([P, 512], F32, tag="t", name="pa")
         nc.tensor.transpose(out=pa[:, 0:P], in_=pmax[:, 0:1].to_broadcast([P, P]), identity=ident[:])

@@ -334,6 +334,7 @@ def tile_multiheadedattention_pa_kernel(tc, x, w, b, out_0, out_1):
             mm(2 * i + 3)
         absmax(out_sb[:, PM0 + 4 : PM0 + 5], 512 * 8, 512 * 10)
         prod(12)
+        back(12)
         evac(11)
         store(5)
         quant(7, 0)
@@ -341,28 +342,27 @@ def tile_multiheadedattention_pa_kernel(tc, x, w, b, out_0, out_1):
         zbias(13)
         mm(14)
         mm(15)
-        back(12)
         gprod(13, 0, 256, True)
         gprod(13, 256, 512, False)
+        evac(12)
         absmax(out_sb[:, PM0 + 5 : PM0 + 6], 512 * 10, 512 * 12)
         prod(14)
         zbias(15, 256, 512)
-        evac(12)
         prod(15, 0, 256)
         gprod(15, 256, 512, False)
         back(13, 0, 256)
-        back(14)
         back(13, 256, 512)
+        back(14)
         evac(13, 0, 256)
-        absmax(out_sb[:, PM0 + 6 : PM0 + 7], 512 * 12, 512 * 13)
-        evac(14)
         evac(13, 256, 512)
-        store(6)
+        absmax(out_sb[:, PM0 + 6 : PM0 + 7], 512 * 12, 512 * 13)
         back(15, 0, 256)
-        absmax(out_sb[:, PM0 + 7 : PM0 + 8], 512 * 14, 512 * 15)
-        evac(15, 0, 256)
+        evac(14)
+        store(6)
+        absmax(out_sb[:, PM0 + 7 : PM0 + 8], 512 * 13, 512 * 14)
         back(15, 256, 512)
-        absmax(out_sb[:, PM0 + 8 : PM0 + 9], 512 * 13, 512 * 14)
+        evac(15, 0, 256)
+        absmax(out_sb[:, PM0 + 8 : PM0 + 9], 512 * 14, 512 * 15)
         evac(15, 256, 512)
         store(7)
         absmax(out_sb[:, PM0 + 9 : PM0 + 10], 512 * 15, 512 * 15 + 256)

@@ -22,7 +22,7 @@ UNITS = 8
 HEADS = 16
 W_RANGES = ((0, 256), (256, 256), (512, 256), (768, 256), (1024, 512), (1536, 512))
 V_SHARE = 336
-CAST_GROUPS = ((0, 2), (2, 2), (4, 4), (8, 4), (12, 4))
+CAST_GROUPS = ((0, 1), (1, 3), (4, 4), (8, 4), (12, 3), (15, 1))
 TWO_PI = 6.283185307179586
 
 

@@ -306,11 +306,10 @@ def tile_multiheadedattention_pa_kernel(tc, x, w, b, out_0, out_1):
         mm_pass(0, 3)
         mm_pass(1, 2)
         mm_pass(1, 3)
-        il("G", 1, 2, 128, 256)
+        il("V", 1, 2, 0, 256)
         il("G", 1, 3, 0, 256)
         il("S", 1, 0, 0, 256)
         il("S", 1, 1, 0, 256)
-        il("S", 1, 2, 0, 128)
 
         for i in range(6):
             if i >= 2:

@@ -322,12 +322,13 @@ def tile_multiheadedattention_pa_kernel(tc, x, w, b, out_0, out_1):
             il("S", i + 2, 0, 0, 256)
             quant(i + 1, 0)
             quant(i + 1, 1)
-            il("G", i + 2, 2, 128, 256)
+            if i >= 1:
+                il("G", i + 2, 2, 128, 256)
             il("G", i + 2, 3, 0, 256)
             mm(2 * i + 2)
             il("S", i + 2, 1, 0, 256)
             evac(2 * i)
-            il("S", i + 2, 2, 0, 128)
+            il("S", i + 2, 2, 0, 128 if i >= 1 else 256)
             prod(2 * i + 1)
             back(2 * i + 1)
             mm(2 * i + 3)
@@ -338,34 +339,37 @@ def tile_multiheadedattention_pa_kernel(tc, x, w, b, out_0, out_1):
         store(5)
         quant(7, 0)
         quant(7, 1)
-        zbias(13)
+        zbias(13, 256, 512)
         mm(14)
         mm(15)
-        gprod(13, 0, 256, True)
+        prod(13, 0, 256)
         gprod(13, 256, 512, False)
         evac(12)
         absmax(out_sb[:, PM0 + 5 : PM0 + 6], 512 * 10, 512 * 12)
-        prod(14)
-        zbias(15, 256, 512)
+        prod(14, 0, 256)
+        zbias(14, 256, 512)
+        gprod(14, 256, 512, False)
         prod(15, 0, 256)
-        gprod(15, 256, 512, False)
+        prod(15, 256, 512)
         back(13, 0, 256)
         back(13, 256, 512)
-        back(14)
+        back(14, 0, 256)
         evac(13, 0, 256)
         evac(13, 256, 512)
+        store(6)
         absmax(out_sb[:, PM0 + 6 : PM0 + 7], 512 * 12, 512 * 13)
         back(15, 0, 256)
-        evac(14)
-        store(6)
-        absmax(out_sb[:, PM0 + 7 : PM0 + 8], 512 * 13, 512 * 14)
+        evac(14, 0, 256)
+        absmax(out_sb[:, PM0 + 7 : PM0 + 8], 512 * 13, 512 * 14 + 256)
         back(15, 256, 512)
         evac(15, 0, 256)
-        absmax(out_sb[:, PM0 + 8 : PM0 + 9], 512 * 14, 512 * 15)
         evac(15, 256, 512)
+        back(14, 256, 512)
+        absmax(out_sb[:, PM0 + 8 : PM0 + 9], 512 * 15, 512 * 16)
+        evac(14, 256, 512)
         store(7)
-        absmax(out_sb[:, PM0 + 9 : PM0 + 10], 512 * 15, 512 * 15 + 256)
-        absmax(pmax[:], 512 * 15 + 256, PM0 + 10)
+        absmax(out_sb[:, PM0 + 9 : PM0 + 10], 512 * 14 + 256, 512 * 15)
+        absmax(pmax[:], PM0, PM0 + 10)
 
         pa = psum.tile([P, 512], F32, tag="t", name="pa")
         nc.tensor.transpose(out=pa[:, 0:P], in_=pmax[:, 0:1].to_broadcast([P, P]), identity=ident[:])

@@ -210,10 +210,10 @@ def tile_multiheadedattention_pa_kernel(tc, x, w, b, out_0, out_1):
         def evac(h, lo=0, hi=512):
             nc.scalar.copy(out=out_sb[:, 512 * h + lo : 512 * h + hi], in_=ot[(h, lo)][:, 0 : hi - lo])
 
-        def store(u):
+        def store(u, n=1):
             nc.sync.dma_start(
-                out=o0v[:, 2 * u : 2 * u + 2, :],
-                in_=out_sb[:, 1024 * u : 1024 * (u + 1)].rearrange("p (h f) -> p h f", h=2),
+                out=o0v[:, 2 * u : 2 * (u + n), :],
+                in_=out_sb[:, 1024 * u : 1024 * (u + n)].rearrange("p (h f) -> p h f", h=2 * n),
             )
 
         def absmax(dst, lo, hi):
@@ -318,7 +318,8 @@ def tile_multiheadedattention_pa_kernel(tc, x, w, b, out_0, out_1):
             back(2 * i)
             if i >= 1:
                 evac(2 * i - 1)
-                store(i - 1)
+                if i == 4:
+                    store(0, 4)
             il("S", i + 2, 0, 0, 256)
             quant(i + 1, 0)
             quant(i + 1, 1)
@@ -336,7 +337,7 @@ def tile_multiheadedattention_pa_kernel(tc, x, w, b, out_0, out_1):
         prod(12)
         back(12)
         evac(11)
-        store(5)
+        store(4, 2)
         quant(7, 0)
         quant(7, 1)
         zbias(13, 256, 512)

@@ -259,8 +259,12 @@ def tile_multiheadedattention_pa_kernel(tc, x, w, b, out_0, out_1):
         def gprod(h, lo, hi, fresh):
             if fresh:
                 prod_t[h] = work.tile([P, 2, 512], F32, tag="at", name="at_%d" % h, bufs=4)
-            for k in range(2):
-                nc.gpsimd.tensor_tensor(out=prod_t[h][:, k, lo:hi], in0=zb[h][:, lo:hi], in1=tab[:, k, lo:hi], op=ALU.mult)
+            nc.gpsimd.tensor_tensor(
+                out=prod_t[h][:, :, lo:hi],
+                in0=zb[h][:, lo:hi].unsqueeze(1).to_broadcast([P, 2, hi - lo]),
+                in1=tab[:, :, lo:hi],
+                op=ALU.mult,
+            )
 
         for a in range(2):
             for g in range(PASSES):

@@ -344,16 +344,16 @@ def tile_multiheadedattention_pa_kernel(tc, x, w, b, out_0, out_1):
         store(4, 2)
         quant(7, 0)
         quant(7, 1)
-        zbias(13, 256, 512)
+        zbias(13, 128, 512)
         mm(14)
         mm(15)
-        prod(13, 0, 256)
-        gprod(13, 256, 512, False)
+        prod(13, 0, 128)
+        gprod(13, 128, 512, False)
         evac(12)
         absmax(out_sb[:, PM0 + 5 : PM0 + 6], 512 * 10, 512 * 12)
-        prod(14, 0, 256)
-        zbias(14, 256, 512)
-        gprod(14, 256, 512, False)
+        prod(14, 0, 384)
+        zbias(14, 384, 512)
+        gprod(14, 384, 512, False)
         prod(15, 0, 256)
         prod(15, 256, 512)
         back(13, 0, 256)

@@ -164,6 +164,13 @@ def tile_multiheadedattention_pa_kernel(tc, x, w, b, out_0, out_1):
                 in_=wg[(u, half)][:].rearrange("p g c j -> p (g c j)"),
             )
 
+        def quant_pass(u, g):
+            nc.vector.quantize_mx(
+                out=wq[u][:, g, :].bitcast(FP8X4),
+                scales=wsc[u][:, g, :],
+                in_=wg[(u, g // 2)][:, g % 2].rearrange("p c j -> p (c j)"),
+            )
+
         def mm_open(h):
             zt[h] = psum.tile([P, 512], F32, tag="z", name="z%d" % h)
 
@@ -290,6 +297,7 @@ def tile_multiheadedattention_pa_kernel(tc, x, w, b, out_0, out_1):
         mm_open(1)
         nc.scalar.activation(out=tab[:, 1, :], in_=tg[:], func=ACT.Sin, scale=TWO_PI)
         nc.scalar.activation(out=tab[:, 0, :], in_=ta[:], func=ACT.Sin, scale=-TWO_PI, bias=TWO_PI / 4.0)
+        nc.vector.tensor_copy(out=bias[:], in_=pc2[:, 0:HEADS])
         x_evac(0, 1)
         il("V", 0, 2, 0, 256)
         x_quant(0, 1)
@@ -300,15 +308,15 @@ def tile_multiheadedattention_pa_kernel(tc, x, w, b, out_0, out_1):
         x_quant(1, 1)
         mm_pass(0, 1)
         mm_pass(1, 1)
+        quant_pass(0, 2)
         x_evac(2, 1)
         x_quant(2, 1)
+        mm_pass(0, 2)
+        mm_pass(1, 2)
         x_evac(3, 1)
         x_quant(3, 1)
-        nc.vector.tensor_copy(out=bias[:], in_=pc2[:, 0:HEADS])
-        quant(0, 1)
-        mm_pass(0, 2)
+        quant_pass(0, 3)
         mm_pass(0, 3)
-        mm_pass(1, 2)
         mm_pass(1, 3)
         il("V", 1, 2, 0, 256)
         il("G", 1, 3, 0, 256)

from contextlib import ExitStack

import concourse.mybir as mybir
from concourse.masks import make_identity

FLOPS = 2 * 512 * 2048 * 2048

F32 = mybir.dt.float32
BF16 = mybir.dt.bfloat16
I32 = mybir.dt.int32
U32 = mybir.dt.uint32
U8 = mybir.dt.uint8
FP8X4 = mybir.dt.float8_e4m3fn_x4
FP8 = mybir.dt.float8_e4m3fn
ALU = mybir.AluOpType
ACT = mybir.ActivationFunctionType
AX = mybir.AxisListType

P = 128
PASSES = 4
UNITS = 8
HEADS = 16
W_RANGES = ((0, 256), (256, 256), (512, 256), (768, 256), (1024, 512), (1536, 512))
V_SHARE = 336
CAST_GROUPS = ((0, 1), (1, 3), (4, 4), (8, 4), (12, 3), (15, 1))
TWO_PI = 6.283185307179586


def tile_multiheadedattention_pa_kernel(tc, x, w, b, out_0, out_1):
    nc = tc.nc
    with ExitStack() as ctx:
        const = ctx.enter_context(tc.tile_pool(name="const", bufs=1))
        work = ctx.enter_context(tc.tile_pool(name="work", bufs=2))
        psum = ctx.enter_context(tc.psum_pool(name="psum", bufs=4))
        ctx.enter_context(tc.manual_schedule())

        xv = x[0].rearrange("(r a) k -> r a k", a=4)
        o0v = out_0[0].rearrange("h (r a) j -> r h (a j)", a=4)
        o1v = out_1[0].rearrange("h (r a) j -> r h (a j)", a=4)

        wraw = {}
        xs = {}

        def load_w(c0, width, g):
            t = const.tile([P, 4, width], BF16, name="wr%d_%d" % (c0, g))
            nc.sync.dma_start(
                out=t[:],
                in_=w[512 * g : 512 * (g + 1), c0 : c0 + width].rearrange("(p j) n -> p j n", j=4),
            )
            wraw[(c0, g)] = t

        def load_x(a):
            t = const.tile([P, 2048], BF16, name="xs%d" % a)
            nc.sync.dma_start(out=t[:], in_=xv[:, a, :])
            xs[a] = t

        b16 = const.tile([16, P], BF16, name="b16")
        nc.sync.dma_start(out=b16[:], in_=b.rearrange("(h c) -> h c", c=P))
        load_x(0)
        load_x(1)
        load_w(0, 256, 0)
        load_w(0, 256, 1)
        load_x(2)
        load_x(3)
        load_w(0, 256, 2)
        load_w(0, 256, 3)
        for c0, width in W_RANGES[1:]:
            for g in range(PASSES):
                load_w(c0, width, g)

        def raw(u, g, lo, hi):
            col = 256 * u
            for c0, width in W_RANGES:
                if c0 <= col < c0 + width:
                    return wraw[(c0, g)][:, :, col - c0 + lo : col - c0 + hi]
            return None

        ident = const.tile([P, P], F32, name="ident")
        swap = const.tile([P, P], F32, name="swap")
        m_idx = const.tile([P, 512], I32, name="m_idx")
        zero = const.tile([P, 1], F32, name="zero")
        warm = const.tile([P, 1], F32, name="warm")
        freq = const.tile([P, P], F32, name="freq")
        turns = const.tile([P, P], F32, name="turns")
        b32 = const.tile([P, P], F32, name="b32")
        ucol = const.tile([P, 1], F32, name="ucol")
        bias = const.tile([P, HEADS], F32, name="bias")
        tk = const.tile([P, 512], I32, name="tk")
        tg = const.tile([P, 512], F32, name="tg")
        ta = const.tile([P, 512], F32, name="ta")
        tab = const.tile([P, 2, 512], F32, name="tab")
        out_sb = const.tile([P, HEADS * 512 + 16], F32, name="out_sb")
        o8 = const.tile([P, HEADS * 512], FP8, name="o8")
        pmax = const.tile([P, 1], F32, name="pmax")
        junk = const.tile([P, P], F32, name="junk")
        scl = const.tile([P, 1], F32, name="scl")
        fac = const.tile([P, 1], F32, name="fac")
        PM0 = HEADS * 512

        make_identity(nc, ident[:])
        nc.gpsimd.iota(m_idx[:], pattern=[[1, 4], [4, P]], base=0, channel_multiplier=0)

        nc.vector.memset(zero[:], 0.0)
        nc.scalar.activation(out=warm[:], in_=zero[:], func=ACT.Sin)
        nc.vector.memset(freq[:, 0:1], 1.0)
        nc.vector.memset(freq[:, 1:2], -1.0)
        for s in range(6):
            n = 2 << s
            nc.vector.tensor_scalar(
                out=freq[:, n : 2 * n], in0=freq[:, 0:n],
                scalar1=10000.0 ** (-(n // 2) / 64.0), scalar2=None, op0=ALU.mult,
            )
        nc.vector.tensor_scalar(out=turns[:], in0=freq[:], scalar1=1.0 / TWO_PI, scalar2=None, op0=ALU.mult)
        pc = psum.tile([P, 512], F32, tag="t", name="pc")
        nc.tensor.transpose(out=pc[:, 0:P], in_=turns[:], identity=ident[:])
        nc.vector.memset(b32[:], 0.0)
        idv = ident[:].rearrange("p (i e) -> p i e", e=2)
        swv = swap[:].rearrange("p (i e) -> p i e", e=2)
        nc.vector.tensor_copy(out=swv[:, :, 0:1], in_=idv[:, :, 1:2])
        nc.vector.tensor_copy(out=swv[:, :, 1:2], in_=idv[:, :, 0:1])
        nc.vector.tensor_copy(out=ucol[:], in_=pc[:, 0:1])
        nc.vector.tensor_scalar(out=tk[:], in0=m_idx[:], scalar1=ucol[:, 0:1], scalar2=None, op0=ALU.mult)
        nc.vector.scalar_tensor_tensor(out=tg[:], in0=m_idx[:], scalar=ucol[:, 0:1], in1=tk[:],
                                       op0=ALU.mult, op1=ALU.subtract)
        nc.vector.scalar_tensor_tensor(out=ta[:], in0=tg[:], scalar=-1.0, in1=tg[:], op0=ALU.mult, op1=ALU.max)
        nc.vector.tensor_copy(out=b32[0:16, :], in_=b16[:])

        wg = {}
        wq = {}
        wsc = {}
        zt = {}
        prod_t = {}
        ot = {}
        xt = {}
        xg = {}
        xq = {}
        xsc = {}

        def il(eng, u, g, lo, hi):
            half = g // 2
            if (u, half) not in wg:
                wg[(u, half)] = work.tile([P, 2, 256, 4], BF16, tag="wg%d" % half, name="wg%d_%d" % (half, u),
                                          bufs=(2 if half == 0 else 1), align_bytes=64)
            if eng == "G":
                src = raw(u, g, lo, hi).rearrange("p j c -> p c j")
                dst = wg[(u, half)][:, g % 2, lo:hi, :]
            else:
                src = raw(u, g, lo, hi).rearrange("p j (c i) -> p c j i", i=4)
                dst = wg[(u, half)][:, g % 2, lo:hi, :].rearrange("p (c i) j -> p c j i", i=4)
            if eng == "S":
                nc.scalar.copy(out=dst, in_=src)
            elif eng == "G":
                nc.gpsimd.tensor_scalar(out=dst, in0=src, scalar1=1.0, scalar2=0.0, op0=ALU.mult, op1=ALU.add)
            else:
                nc.vector.tensor_copy(out=dst, in_=src)

        def quant(u, half):
            if half == 0:
                wq[u] = work.tile([P, PASSES, 256], U32, tag="wq", name="wq%d" % u, bufs=3, align_bytes=64)
                wsc[u] = work.tile([P, PASSES, 256], U8, tag="wsc", name="wsc%d" % u, bufs=3, align_bytes=64)
            nc.vector.quantize_mx(
                out=wq[u][:, 2 * half : 2 * half + 2, :].rearrange("p g c -> p (g c)").bitcast(FP8X4),
                scales=wsc[u][:, 2 * half : 2 * half + 2, :].rearrange("p g c -> p (g c)"),
                in_=wg[(u, half)][:].rearrange("p g c j -> p (g c j)"),
            )

        def quant_pass(u, g):
            nc.vector.quantize_mx(
                out=wq[u][:, g, :].bitcast(FP8X4),
                scales=wsc[u][:, g, :],
                in_=wg[(u, g // 2)][:, g % 2].rearrange("p c j -> p (c j)"),
            )

        def mm_open(h):
            zt[h] = psum.tile([P, 512], F32, tag="z", name="z%d" % h)

        def mm_pass(h, g):
            u = h // 2
            hh = h % 2
            nc.tensor.matmul_mx(
                out=zt[h][:],
                lhsT=wq[u][:, g, P * hh : P * (hh + 1)].bitcast(FP8X4),
                lhsT_scale=wsc[u][:, g, P * hh : P * (hh + 1)],
                rhs=xq[g][:].bitcast(FP8X4),
                rhs_scale=xsc[g][:],
                start=(g == 0),
                stop=(g == PASSES - 1),
            )

        def mm(h):
            mm_open(h)
            for g in range(PASSES):
                mm_pass(h, g)

        def prod(h, lo=0, hi=512):
            if lo == 0:
                prod_t[h] = work.tile([P, 2, 512], F32, tag="at", name="at_%d" % h, bufs=4)
            nc.vector.scalar_tensor_tensor(
                out=prod_t[h][:, :, lo:hi],
                in0=zt[h][:, lo:hi].unsqueeze(1).to_broadcast([P, 2, hi - lo]),
                scalar=bias[:, h : h + 1],
                in1=tab[:, :, lo:hi],
                op0=ALU.add,
                op1=ALU.mult,
            )

        def back(h, lo=0, hi=512):
            o = psum.tile([P, 512], F32, tag="t", name="o%d_%d" % (h, lo))
            ot[(h, lo)] = o
            at = prod_t[h]
            for c in range(lo, hi, P):
                nc.tensor.matmul(out=o[:, c - lo : c - lo + P], lhsT=at[:, 0, c : c + P], rhs=ident[:], start=True,
                                 stop=False, is_transpose=True)
                nc.tensor.matmul(out=o[:, c - lo : c - lo + P], lhsT=at[:, 1, c : c + P], rhs=swap[:], start=False,
                                 stop=True, is_transpose=True)

        def evac(h, lo=0, hi=512):
            nc.scalar.copy(out=out_sb[:, 512 * h + lo : 512 * h + hi], in_=ot[(h, lo)][:, 0 : hi - lo])

        def store(u, n=1):
            nc.sync.dma_start(
                out=o0v[:, 2 * u : 2 * (u + n), :],
                in_=out_sb[:, 1024 * u : 1024 * (u + n)].rearrange("p (h f) -> p h f", h=2 * n),
            )

        def absmax(dst, lo, hi):
            nc.vector.tensor_reduce(out=dst, in_=out_sb[:, lo:hi], axis=AX.X, op=ALU.max,
                                    apply_absolute_value=True)

        def x_transposes(a, g):
            ap = a // 2
            a2 = a % 2
            if a2 == 0:
                xt[(g, ap)] = psum.tile([P, 512], F32, tag="t", name="xt%d_%d" % (g, ap))
            words = xs[a][:, 512 * g : 512 * (g + 1)].bitcast(F32)
            for uu in range(2):
                k = 2 * a2 + uu
                nc.tensor.transpose(out=xt[(g, ap)][:, P * k : P * (k + 1)], in_=words[:, uu:256:2],
                                    identity=ident[:])

        def x_evac(g, ap):
            xg[(g, ap)] = work.tile([P, 1024], BF16, tag="xg", name="xg%d_%d" % (g, ap), bufs=3, align_bytes=64)
            dst = xg[(g, ap)][:].bitcast(F32).rearrange("p (a r u) -> p a r u", a=2, u=2)
            src = xt[(g, ap)][:].rearrange("p (a u r) -> p a r u", a=2, u=2)
            nc.scalar.copy(out=dst, in_=src)

        def x_quant(g, ap):
            if ap == 0:
                xq[g] = const.tile([P, 512], U32, name="xq%d" % g, align_bytes=64)
                xsc[g] = const.tile([P, 512], U8, name="xsc%d" % g, align_bytes=64)
            nc.vector.quantize_mx(out=xq[g][:, 256 * ap : 256 * (ap + 1)].bitcast(FP8X4),
                                  scales=xsc[g][:, 256 * ap : 256 * (ap + 1)], in_=xg[(g, ap)][:])

        def dummies(n, name):
            d = psum.tile([P, 512], F32, tag="z", name=name)
            for k in range(n):
                nc.tensor.matmul(out=d[:, 0:P], lhsT=ident[:], rhs=ident[:], start=True, stop=True)

        zb = {}

        def zbias(h, lo=0, hi=512):
            zb[h] = work.tile([P, 512], F32, tag="zb", name="zb%d" % h, bufs=2)
            nc.scalar.activation(out=zb[h][:, lo:hi], in_=zt[h][:, lo:hi], func=ACT.Identity, bias=bias[:, h : h + 1],
                                 scale=1.0)

        def gprod(h, lo, hi, fresh):
            if fresh:
                prod_t[h] = work.tile([P, 2, 512], F32, tag="at", name="at_%d" % h, bufs=4)
            nc.gpsimd.tensor_tensor(
                out=prod_t[h][:, :, lo:hi],
                in0=zb[h][:, lo:hi].unsqueeze(1).to_broadcast([P, 2, hi - lo]),
                in1=tab[:, :, lo:hi],
                op=ALU.mult,
            )

        for a in range(2):
            for g in range(PASSES):
                x_transposes(a, g)
        pc2 = psum.tile([P, 512], F32, tag="z", name="pc2")
        nc.tensor.transpose(out=pc2[:, 0:P], in_=b32[:], identity=ident[:])
        il("V", 0, 0, 0, 256)
        x_evac(0, 0)
        x_quant(0, 0)
        x_evac(1, 0)
        x_quant(1, 0)
        il("V", 0, 1, 0, 256)
        x_evac(2, 0)
        x_quant(2, 0)
        x_evac(3, 0)
        x_quant(3, 0)
        quant(0, 0)
        for a in range(2, 4):
            for g in range(PASSES):
                x_transposes(a, g)
        dummies(3, "dz0")
        mm_open(0)
        mm_open(1)
        nc.scalar.activation(out=tab[:, 1, :], in_=tg[:], func=ACT.Sin, scale=TWO_PI)
        nc.scalar.activation(out=tab[:, 0, :], in_=ta[:], func=ACT.Sin, scale=-TWO_PI, bias=TWO_PI / 4.0)
        nc.vector.tensor_copy(out=bias[:], in_=pc2[:, 0:HEADS])
        x_evac(0, 1)
        il("V", 0, 2, 0, 256)
        x_quant(0, 1)
        mm_pass(0, 0)
        mm_pass(1, 0)
        x_evac(1, 1)
        il("V", 0, 3, 0, 256)
        x_quant(1, 1)
        mm_pass(0, 1)
        mm_pass(1, 1)
        quant_pass(0, 2)
        x_evac(2, 1)
        x_quant(2, 1)
        mm_pass(0, 2)
        mm_pass(1, 2)
        x_evac(3, 1)
        x_quant(3, 1)
        quant_pass(0, 3)
        mm_pass(0, 3)
        mm_pass(1, 3)
        il("V", 1, 2, 0, 256)
        il("G", 1, 3, 0, 256)
        il("S", 1, 0, 0, 256)
        il("S", 1, 1, 0, 256)

        for i in range(6):
            if i >= 2:
                absmax(out_sb[:, PM0 + i - 2 : PM0 + i - 1], 512 * (2 * i - 4), 512 * (2 * i - 2))
            prod(2 * i)
            back(2 * i)
            if i >= 1:
                evac(2 * i - 1)
                if i == 4:
                    store(0, 4)
            il("S", i + 2, 0, 0, 256)
            quant(i + 1, 0)
            quant(i + 1, 1)
            if i >= 1:
                il("G", i + 2, 2, 128, 256)
            il("G", i + 2, 3, 0, 256)
            mm(2 * i + 2)
            il("S", i + 2, 1, 0, 256)
            evac(2 * i)
            il("S", i + 2, 2, 0, 128 if i >= 1 else 256)
            prod(2 * i + 1)
            back(2 * i + 1)
            mm(2 * i + 3)
        absmax(out_sb[:, PM0 + 4 : PM0 + 5], 512 * 8, 512 * 10)
        prod(12)
        back(12)
        evac(11)
        store(4, 2)
        quant(7, 0)
        quant(7, 1)
        zbias(13, 128, 512)
        mm(14)
        mm(15)
        prod(13, 0, 128)
        gprod(13, 128, 512, False)
        evac(12)
        absmax(out_sb[:, PM0 + 5 : PM0 + 6], 512 * 10, 512 * 12)
        prod(14, 0, 384)
        zbias(14, 384, 512)
        gprod(14, 384, 512, False)
        prod(15, 0, 256)
        prod(15, 256, 512)
        back(13, 0, 256)
        back(13, 256, 512)
        back(14, 0, 256)
        evac(13, 0, 256)
        evac(13, 256, 512)
        store(6)
        absmax(out_sb[:, PM0 + 6 : PM0 + 7], 512 * 12, 512 * 13)
        back(15, 0, 256)
        evac(14, 0, 256)
        absmax(out_sb[:, PM0 + 7 : PM0 + 8], 512 * 13, 512 * 14 + 256)
        back(15, 256, 512)
        evac(15, 0, 256)
        evac(15, 256, 512)
        back(14, 256, 512)
        absmax(out_sb[:, PM0 + 8 : PM0 + 9], 512 * 15, 512 * 16)
        evac(14, 256, 512)
        store(7)
        absmax(out_sb[:, PM0 + 9 : PM0 + 10], 512 * 14 + 256, 512 * 15)
        absmax(pmax[:], PM0, PM0 + 10)

        pa = psum.tile([P, 512], F32, tag="t", name="pa")
        nc.tensor.transpose(out=pa[:, 0:P], in_=pmax[:, 0:1].to_broadcast([P, P]), identity=ident[:])
        nc.vector.tensor_scalar(out=junk[:], in0=pa[:, 0:P], scalar1=1.0 / 448.0, scalar2=None, op0=ALU.mult,
                                op1=ALU.max, accum_out=scl[:, 0:1])
        nc.vector.reciprocal(out=fac[:], in_=scl[:])
        for h0, nh in CAST_GROUPS:
            lo = 512 * h0
            mid = lo + V_SHARE * nh
            hi = lo + 512 * nh
            nc.vector.tensor_scalar(out=o8[:, lo:mid], in0=out_sb[:, lo:mid], scalar1=fac[:, 0:1], scalar2=None,
                                    op0=ALU.mult, saturate=False)
            nc.scalar.activation(out=o8[:, mid:hi], in_=out_sb[:, mid:hi], func=ACT.Identity, scale=fac[:, 0:1],
                                 bias=zero[:, 0:1], saturate=False)
            nc.sync.dma_start(
                out=o1v[:, h0 : h0 + nh, :],
                in_=o8[:, lo:hi].bitcast(U8).rearrange("p (h f) -> p h f", h=nh),
            )
